import numpy as np
import ml_dtypes


def mxq(x, axis, fmt="e4m3"):
    dtype, down = {"e4m3": (ml_dtypes.float8_e4m3fn, 7), "e5m2": (ml_dtypes.float8_e5m2, 14)}[fmt]
    v = np.moveaxis(np.asarray(x, np.float32).astype(ml_dtypes.bfloat16).astype(np.float64), axis, -1)
    blocks = v.reshape(v.shape[:-1] + (-1, 32))
    amax = np.abs(blocks).max(-1, keepdims=True)
    byte = np.maximum(np.where(amax > 0, np.frexp(amax)[1] - 1 + 127, 0) - down, 1)
    scale = np.exp2(byte - 127.0)
    codes = (blocks / scale).astype(np.float32).astype(dtype).astype(np.float64)
    return np.moveaxis((codes * scale).reshape(v.shape), -1, axis)


WIDE = False


def mx_kscale(k):
    if not WIDE:
        return np.ones(k)
    levels = np.array([10, -10, 5, -5, 0])
    a = np.random.permutation(np.resize(levels, k // 512 * 4)).reshape(k // 512, 4)
    idx = np.arange(k)
    return np.exp2(a[idx // 512, idx % 128 // 32])


BF16 = ml_dtypes.bfloat16


def bf(x):
    return np.asarray(x, np.float32).astype(BF16)


def f64(x):
    return np.asarray(x).astype(np.float64)


L, N, E, H, C, LW, RW = 8192, 1, 512, 8, 512, 1, 1
EPS = 1e-8


def sigmoid(v):
    return 1.0 / (1.0 + np.exp(-v))


def setup_inputs():
    s = mx_kscale(E)
    return {"attn_out": bf(np.random.standard_normal((L, N, E)) * 2.0),
            "norm_scale": bf((1.0 + 0.1 * np.random.standard_normal(E)) * s),
            "norm_gate": bf(1.0 + 0.2 * np.random.standard_normal(E)),
            "w_o": bf(np.random.standard_normal((E, E)) / np.sqrt(E) / s[None, :]),
            "b_o": bf(np.random.standard_normal(E) * 0.1)}


def reference(attn_out, norm_scale, norm_gate, w_o, b_o):
    x = f64(attn_out)
    rms = np.sqrt(np.mean(x * x, axis=-1, keepdims=True))
    y = f64(norm_scale) * (x / (rms + EPS)) * sigmoid(f64(norm_gate) * x)
    return (mxq(y, 2, "e4m3") @ mxq(f64(w_o), 1, "e4m3").T) + f64(b_o)

@@ -1,0 +1,189 @@
+from contextlib import ExitStack
+import math
+
+import concourse.mybir as mybir
+from concourse.masks import make_identity
+
+FLOPS = 2 * 8192 * 512 * 512
+
+BF16 = mybir.dt.bfloat16
+F32 = mybir.dt.float32
+U32 = mybir.dt.uint32
+U8 = mybir.dt.uint8
+FP8X4 = mybir.dt.float8_e4m3fn_x4
+ACT = mybir.ActivationFunctionType
+ALU = mybir.AluOpType
+
+P = 128
+PACK = 4
+FEATURES = P * PACK
+OUT_FEATURES = 512
+TILES = 4
+GROUP = TILES * P
+EPS = 1e-8
+GATE_FLOOR = 2.0**-64
+
+
+def tile_normlocalattention_pb_t_kernel(tc, attn_out, norm_scale, norm_gate, w_o, b_o, out):
+    nc = tc.nc
+    x_rows = attn_out.flatten_outer_dims()
+    out_rows = out.flatten_outer_dims()
+    tokens = x_rows.shape[0]
+    groups = tokens // GROUP
+
+    with ExitStack() as stack:
+        const = stack.enter_context(tc.tile_pool(name="const", bufs=1))
+        x_pool = stack.enter_context(tc.tile_pool(name="x", bufs=groups))
+        stats = stack.enter_context(tc.tile_pool(name="stats", bufs=4))
+        work = stack.enter_context(tc.tile_pool(name="work", bufs=3))
+        results = stack.enter_context(tc.tile_pool(name="results", bufs=4))
+        psum_words = stack.enter_context(tc.psum_pool(name="psum_words", bufs=4))
+        psum_inv = stack.enter_context(tc.psum_pool(name="psum_inv", bufs=2))
+        psum_acc = stack.enter_context(tc.psum_pool(name="psum_acc", bufs=2))
+
+        gate_bf = const.tile([P, PACK], BF16)
+        scale_bf = const.tile([P, PACK], BF16)
+        nc.scalar.dma_start(
+            out=gate_bf[:].rearrange("p (u e) -> p u e", e=2),
+            in_=norm_gate.rearrange("(u p e) -> p u e", u=2, e=2),
+        )
+        nc.scalar.dma_start(
+            out=scale_bf[:].rearrange("p (u e) -> p u e", e=2),
+            in_=norm_scale.rearrange("(u p e) -> p u e", u=2, e=2),
+        )
+        w_rows = const.tile([P, OUT_FEATURES // P, FEATURES], BF16)
+        nc.scalar.dma_start(out=w_rows[:], in_=w_o.rearrange("(c p) k -> p c k", p=P))
+        bias = const.tile([P, OUT_FEATURES], BF16)
+        nc.scalar.dma_start(out=bias[:], in_=b_o.partition_broadcast(P))
+
+        x_tiles = []
+        for g in range(groups):
+            x_tile = x_pool.tile([P, TILES, FEATURES], BF16, name="x_tile")
+            nc.sync.dma_start(
+                out=x_tile[:],
+                in_=x_rows[g * GROUP : (g + 1) * GROUP, :].rearrange("(p j) k -> p j k", j=TILES),
+            )
+            x_tiles.append(x_tile)
+
+        ident = const.tile([P, P], F32)
+        make_identity(nc, ident[:])
+        half = const.tile([P, TILES], F32)
+        nc.vector.memset(half[:], 0.5)
+
+        gate = const.tile([P, PACK], F32)
+        size = const.tile([P, PACK], F32)
+        lift = const.tile([P, PACK], F32)
+        gain = const.tile([P, PACK], F32)
+        nc.vector.tensor_copy(out=gate[:], in_=gate_bf[:])
+        nc.vector.tensor_scalar_mul(out=size[:], in0=gate[:], scalar1=-1.0)
+        nc.vector.tensor_max(out=size[:], in0=size[:], in1=gate[:])
+        nc.vector.tensor_scalar(
+            out=lift[:], in0=size[:], scalar1=GATE_FLOOR, scalar2=GATE_FLOOR, op0=ALU.is_lt, op1=ALU.mult
+        )
+        nc.vector.tensor_add(out=gate[:], in0=gate[:], in1=lift[:])
+        nc.vector.reciprocal(out=gain[:], in_=gate[:])
+        nc.vector.tensor_mul(out=gain[:], in0=gain[:], in1=scale_bf[:])
+
+        w_grouped = const.tile([P, OUT_FEATURES, 2], F32, align_bytes=64)
+        for h in range(2):
+            w_words = psum_words.tile([P, 2, 2 * P], F32, tag="words")
+            for u in range(2):
+                for c in range(2):
+                    nc.tensor.transpose(
+                        w_words[:, u, c * P : (c + 1) * P],
+                        w_rows[:, 2 * h + c, :].bitcast(F32)[:, u * P : (u + 1) * P],
+                        ident[:],
+                    )
+            nc.vector.tensor_copy(
+                out=w_grouped[:, h * 2 * P : (h + 1) * 2 * P, :],
+                in_=w_words[:].rearrange("p u o -> p o u"),
+            )
+        w_codes = const.tile([P, OUT_FEATURES], U32, align_bytes=64)
+        w_scales = const.tile([P, OUT_FEATURES], U8, align_bytes=64)
+        nc.vector.quantize_mx(
+            out=w_codes[:].bitcast(FP8X4),
+            scales=w_scales[:],
+            in_=w_grouped[:].rearrange("p o u -> p (o u)").bitcast(BF16),
+        )
+
+        for g in range(groups):
+            x_tile = x_tiles[g]
+
+            squares = work.tile([P, TILES, FEATURES], BF16)
+            mean_sq = stats.tile([P, TILES], F32)
+            for j in range(TILES):
+                nc.scalar.activation(
+                    out=squares[:, j, :],
+                    in_=x_tile[:, j, :],
+                    func=ACT.Square,
+                    scale=1.0 / math.sqrt(FEATURES),
+                    accum_out=mean_sq[:, j : j + 1],
+                )
+            rms = stats.tile([P, TILES], F32)
+            nc.gpsimd.tensor_tensor(out=rms[:], in0=mean_sq[:], in1=half[:], op=ALU.pow)
+            nc.gpsimd.tensor_scalar(out=rms[:], in0=rms[:], scalar1=EPS, scalar2=1.0, op0=ALU.add, op1=ALU.mult)
+            inv = stats.tile([P, TILES], F32)
+            nc.vector.reciprocal(out=inv[:], in_=rms[:])
+
+            inv_all = psum_inv.tile([P, GROUP], F32)
+            for j in range(TILES):
+                nc.tensor.transpose(
+                    inv_all[:, j * P : (j + 1) * P], inv[:, j : j + 1].to_broadcast([P, P]), ident[:]
+                )
+
+            silu = work.tile([P, PACK, GROUP], F32)
+            for u in range(2):
+                x_words = psum_words.tile([P, GROUP], F32, tag="words")
+                for j in range(TILES):
+                    nc.tensor.transpose(
+                        x_words[:, j * P : (j + 1) * P],
+                        x_tile[:, j, :].bitcast(F32)[:, u * P : (u + 1) * P],
+                        ident[:],
+                    )
+                pairs = x_words[:].bitcast(BF16).rearrange("p (n e) -> p n e", e=2)
+                for e in range(2):
+                    t = 2 * u + e
+                    nc.scalar.activation(
+                        out=silu[:, t, :], in_=pairs[:, :, e], func=ACT.Silu, scale=gate[:, t : t + 1]
+                    )
+
+            y_planes = work.tile([P, PACK, GROUP], BF16)
+            for t in range(PACK):
+                nc.vector.scalar_tensor_tensor(
+                    out=y_planes[:, t, :],
+                    in0=silu[:, t, :],
+                    scalar=gain[:, t : t + 1],
+                    in1=inv_all[:],
+                    op0=ALU.mult,
+                    op1=ALU.mult,
+                )
+            y_grouped = work.tile([P, GROUP, PACK], BF16, align_bytes=64)
+            nc.vector.tensor_copy(
+                out=y_grouped[:].rearrange("p (c i) t -> p c t i", i=4),
+                in_=y_planes[:].rearrange("p t (c i) -> p c t i", i=4),
+            )
+            y_codes = work.tile([P, GROUP], U32, align_bytes=64)
+            y_scales = work.tile([P, GROUP], U8, align_bytes=64)
+            nc.vector.quantize_mx(
+                out=y_codes[:].bitcast(FP8X4),
+                scales=y_scales[:],
+                in_=y_grouped[:].rearrange("p n t -> p (n t)"),
+            )
+
+            result = results.tile([P, TILES, OUT_FEATURES], F32)
+            for j in range(TILES):
+                acc = psum_acc.tile([P, OUT_FEATURES], F32)
+                nc.tensor.matmul_mx(
+                    out=acc[:],
+                    lhsT=y_codes[:, j * P : (j + 1) * P].bitcast(FP8X4),
+                    lhsT_scale=y_scales[:, j * P : (j + 1) * P],
+                    rhs=w_codes[:].bitcast(FP8X4),
+                    rhs_scale=w_scales[:],
+                    start=True,
+                    stop=True,
+                )
+                nc.vector.tensor_tensor(out=result[:, j, :], in0=acc[:], in1=bias[:], op=ALU.add)
+            nc.sync.dma_start(
+                out=out_rows[g * GROUP : (g + 1) * GROUP, :].rearrange("(p j) o -> p j o", j=TILES),
+                in_=result[:],
+            )

@@ -158,9 +158,13 @@ def tile_normlocalattention_pb_t_kernel(tc, attn_out, norm_scale, norm_gate, w_o
                     op1=ALU.mult,
                 )
             y_grouped = work.tile([P, GROUP, PACK], BF16, align_bytes=64)
-            nc.vector.tensor_copy(
-                out=y_grouped[:].rearrange("p (c i) t -> p c t i", i=4),
-                in_=y_planes[:].rearrange("p t (c i) -> p c t i", i=4),
+            nc.gpsimd.tensor_scalar(
+                out=y_grouped[:],
+                in0=y_planes[:].rearrange("p t n -> p n t"),
+                scalar1=1.0,
+                scalar2=0.0,
+                op0=ALU.mult,
+                op1=ALU.add,
             )
             y_codes = work.tile([P, GROUP], U32, align_bytes=64)
             y_scales = work.tile([P, GROUP], U8, align_bytes=64)

@@ -32,14 +32,16 @@ def tile_normlocalattention_pb_t_kernel(tc, attn_out, norm_scale, norm_gate, w_o
     groups = tokens // GROUP
 
     with ExitStack() as stack:
+        stack.enter_context(tc.manual_schedule())
         const = stack.enter_context(tc.tile_pool(name="const", bufs=1))
         x_pool = stack.enter_context(tc.tile_pool(name="x", bufs=groups))
         stats = stack.enter_context(tc.tile_pool(name="stats", bufs=4))
         work = stack.enter_context(tc.tile_pool(name="work", bufs=3))
+        single = stack.enter_context(tc.tile_pool(name="single", bufs=1))
         results = stack.enter_context(tc.tile_pool(name="results", bufs=4))
-        psum_words = stack.enter_context(tc.psum_pool(name="psum_words", bufs=4))
-        psum_inv = stack.enter_context(tc.psum_pool(name="psum_inv", bufs=2))
-        psum_acc = stack.enter_context(tc.psum_pool(name="psum_acc", bufs=2))
+        psum_words = stack.enter_context(tc.psum_pool(name="psum_words", bufs=3))
+        psum_inv = stack.enter_context(tc.psum_pool(name="psum_inv", bufs=1))
+        psum_acc = stack.enter_context(tc.psum_pool(name="psum_acc", bufs=TILES))
 
         gate_bf = const.tile([P, PACK], BF16)
         scale_bf = const.tile([P, PACK], BF16)
@@ -106,88 +108,134 @@ def tile_normlocalattention_pb_t_kernel(tc, attn_out, norm_scale, norm_gate, w_o
             in_=w_grouped[:].rearrange("p o u -> p (o u)").bitcast(BF16),
         )
 
-        for g in range(groups):
-            x_tile = x_tiles[g]
+        rms_of = {}
+        inv_all_of = {}
+        x_words_of = {}
+        silu_of = {}
+        y_planes_of = {}
+        y_grouped_of = {}
+        y_codes_of = {}
+        y_scales_of = {}
+        acc_of = {}
 
-            squares = work.tile([P, TILES, FEATURES], BF16)
-            mean_sq = stats.tile([P, TILES], F32)
+        def root_mean_squares(g):
+            squares = work.tile([P, TILES, FEATURES], BF16, name="squares")
+            mean_sq = stats.tile([P, TILES], F32, name="mean_sq")
             for j in range(TILES):
                 nc.scalar.activation(
                     out=squares[:, j, :],
-                    in_=x_tile[:, j, :],
+                    in_=x_tiles[g][:, j, :],
                     func=ACT.Square,
                     scale=1.0 / math.sqrt(FEATURES),
                     accum_out=mean_sq[:, j : j + 1],
                 )
-            rms = stats.tile([P, TILES], F32)
+            rms = stats.tile([P, TILES], F32, name="rms")
             nc.gpsimd.tensor_tensor(out=rms[:], in0=mean_sq[:], in1=half[:], op=ALU.pow)
             nc.gpsimd.tensor_scalar(out=rms[:], in0=rms[:], scalar1=EPS, scalar2=1.0, op0=ALU.add, op1=ALU.mult)
-            inv = stats.tile([P, TILES], F32)
-            nc.vector.reciprocal(out=inv[:], in_=rms[:])
+            rms_of[g] = rms
 
-            inv_all = psum_inv.tile([P, GROUP], F32)
+        def spread_inverse_rms(g):
+            inv = stats.tile([P, TILES], F32, name="inv")
+            nc.vector.reciprocal(out=inv[:], in_=rms_of[g][:])
+            inv_all = psum_inv.tile([P, GROUP], F32, name="inv_all")
             for j in range(TILES):
                 nc.tensor.transpose(
                     inv_all[:, j * P : (j + 1) * P], inv[:, j : j + 1].to_broadcast([P, P]), ident[:]
                 )
+            inv_all_of[g] = inv_all
 
-            silu = work.tile([P, PACK, GROUP], F32)
+        def transpose_x(g):
             for u in range(2):
-                x_words = psum_words.tile([P, GROUP], F32, tag="words")
+                x_words = psum_words.tile([P, GROUP], F32, name="x_words", tag="words")
                 for j in range(TILES):
                     nc.tensor.transpose(
                         x_words[:, j * P : (j + 1) * P],
-                        x_tile[:, j, :].bitcast(F32)[:, u * P : (u + 1) * P],
+                        x_tiles[g][:, j, :].bitcast(F32)[:, u * P : (u + 1) * P],
                         ident[:],
                     )
-                pairs = x_words[:].bitcast(BF16).rearrange("p (n e) -> p n e", e=2)
+                x_words_of[(g, u)] = x_words
+
+        def gated(g):
+            silu = work.tile([P, PACK, GROUP], F32, name="silu")
+            for u in range(2):
+                pairs = x_words_of[(g, u)][:].bitcast(BF16).rearrange("p (n e) -> p n e", e=2)
                 for e in range(2):
                     t = 2 * u + e
                     nc.scalar.activation(
                         out=silu[:, t, :], in_=pairs[:, :, e], func=ACT.Silu, scale=gate[:, t : t + 1]
                     )
+            silu_of[g] = silu
 
-            y_planes = work.tile([P, PACK, GROUP], BF16)
+        def normed(g):
+            y_planes = work.tile([P, PACK, GROUP], BF16, name="y_planes")
             for t in range(PACK):
                 nc.vector.scalar_tensor_tensor(
                     out=y_planes[:, t, :],
-                    in0=silu[:, t, :],
+                    in0=silu_of[g][:, t, :],
                     scalar=gain[:, t : t + 1],
-                    in1=inv_all[:],
+                    in1=inv_all_of[g][:],
                     op0=ALU.mult,
                     op1=ALU.mult,
                 )
-            y_grouped = work.tile([P, GROUP, PACK], BF16, align_bytes=64)
+            y_planes_of[g] = y_planes
+
+        def regroup(g):
+            y_grouped = single.tile([P, GROUP, PACK], BF16, name="y_grouped", align_bytes=64)
             nc.gpsimd.tensor_scalar(
                 out=y_grouped[:],
-                in0=y_planes[:].rearrange("p t n -> p n t"),
+                in0=y_planes_of[g][:].rearrange("p t n -> p n t"),
                 scalar1=1.0,
                 scalar2=0.0,
                 op0=ALU.mult,
                 op1=ALU.add,
             )
-            y_codes = work.tile([P, GROUP], U32, align_bytes=64)
-            y_scales = work.tile([P, GROUP], U8, align_bytes=64)
+            y_grouped_of[g] = y_grouped
+
+        def quantise(g):
+            y_codes = work.tile([P, GROUP], U32, name="y_codes", align_bytes=64)
+            y_scales = work.tile([P, GROUP], U8, name="y_scales", align_bytes=64)
             nc.vector.quantize_mx(
                 out=y_codes[:].bitcast(FP8X4),
                 scales=y_scales[:],
-                in_=y_grouped[:].rearrange("p n t -> p (n t)"),
+                in_=y_grouped_of[g][:].rearrange("p n t -> p (n t)"),
             )
+            y_codes_of[g] = y_codes
+            y_scales_of[g] = y_scales
 
-            result = results.tile([P, TILES, OUT_FEATURES], F32)
+        def multiply(g):
             for j in range(TILES):
-                acc = psum_acc.tile([P, OUT_FEATURES], F32)
+                acc = psum_acc.tile([P, OUT_FEATURES], F32, name="acc")
                 nc.tensor.matmul_mx(
                     out=acc[:],
-                    lhsT=y_codes[:, j * P : (j + 1) * P].bitcast(FP8X4),
-                    lhsT_scale=y_scales[:, j * P : (j + 1) * P],
+                    lhsT=y_codes_of[g][:, j * P : (j + 1) * P].bitcast(FP8X4),
+                    lhsT_scale=y_scales_of[g][:, j * P : (j + 1) * P],
                     rhs=w_codes[:].bitcast(FP8X4),
                     rhs_scale=w_scales[:],
                     start=True,
                     stop=True,
                 )
-                nc.vector.tensor_tensor(out=result[:, j, :], in0=acc[:], in1=bias[:], op=ALU.add)
+                acc_of[(g, j)] = acc
+
+        def add_bias_and_store(g):
+            result = results.tile([P, TILES, OUT_FEATURES], F32, name="result")
+            for j in range(TILES):
+                nc.vector.tensor_tensor(out=result[:, j, :], in0=acc_of[(g, j)][:], in1=bias[:], op=ALU.add)
             nc.sync.dma_start(
                 out=out_rows[g * GROUP : (g + 1) * GROUP, :].rearrange("(p j) o -> p j o", j=TILES),
                 in_=result[:],
             )
+
+        def run(stage, g):
+            if 0 <= g < groups:
+                stage(g)
+
+        for step in range(-2, groups + 2):
+            run(gated, step + 1)
+            run(transpose_x, step + 2)
+            run(root_mean_squares, step + 2)
+            run(normed, step)
+            run(spread_inverse_rms, step + 1)
+            run(add_bias_and_store, step - 2)
+            run(quantise, step - 1)
+            run(multiply, step - 1)
+            run(regroup, step)

@@ -20,25 +20,37 @@ FEATURES = P * PACK
 OUT_FEATURES = 512
 TILES = 4
 GROUP = TILES * P
+RAMP = (1, 1, 2)
 EPS = 1e-8
 GATE_FLOOR = 2.0**-64
+
+
+def group_sizes(token_tiles):
+    full_groups = (token_tiles - 2 * sum(RAMP)) // TILES
+    sizes = list(RAMP) + [TILES] * full_groups + list(reversed(RAMP))
+    assert sum(sizes) == token_tiles
+    return sizes
 
 
 def tile_normlocalattention_pb_t_kernel(tc, attn_out, norm_scale, norm_gate, w_o, b_o, out):
     nc = tc.nc
     x_rows = attn_out.flatten_outer_dims()
     out_rows = out.flatten_outer_dims()
-    tokens = x_rows.shape[0]
-    groups = tokens // GROUP
+    tiles_of = group_sizes(x_rows.shape[0] // P)
+    groups = len(tiles_of)
+
+    def rows_of_group(rows, g):
+        start = P * sum(tiles_of[:g])
+        return rows[start : start + P * tiles_of[g], :].rearrange("(p j) k -> p j k", j=tiles_of[g])
 
     with ExitStack() as stack:
         stack.enter_context(tc.manual_schedule())
         const = stack.enter_context(tc.tile_pool(name="const", bufs=1))
-        x_pool = stack.enter_context(tc.tile_pool(name="x", bufs=groups))
+        x_pool = stack.enter_context(tc.tile_pool(name="x", bufs=1))
         stats = stack.enter_context(tc.tile_pool(name="stats", bufs=4))
         work = stack.enter_context(tc.tile_pool(name="work", bufs=3))
         single = stack.enter_context(tc.tile_pool(name="single", bufs=1))
-        results = stack.enter_context(tc.tile_pool(name="results", bufs=4))
+        results = stack.enter_context(tc.tile_pool(name="results", bufs=2 * TILES))
         psum_words = stack.enter_context(tc.psum_pool(name="psum_words", bufs=3))
         psum_inv = stack.enter_context(tc.psum_pool(name="psum_inv", bufs=1))
         psum_acc = stack.enter_context(tc.psum_pool(name="psum_acc", bufs=TILES))
@@ -53,24 +65,24 @@ def tile_normlocalattention_pb_t_kernel(tc, attn_out, norm_scale, norm_gate, w_o
             out=scale_bf[:].rearrange("p (u e) -> p u e", e=2),
             in_=norm_scale.rearrange("(u p e) -> p u e", u=2, e=2),
         )
-        w_rows = const.tile([P, OUT_FEATURES // P, FEATURES], BF16)
-        nc.scalar.dma_start(out=w_rows[:], in_=w_o.rearrange("(c p) k -> p c k", p=P))
         bias = const.tile([P, OUT_FEATURES], BF16)
         nc.scalar.dma_start(out=bias[:], in_=b_o.partition_broadcast(P))
 
         x_tiles = []
+        w_rows = const.tile([P, OUT_FEATURES // P, FEATURES], BF16)
         for g in range(groups):
-            x_tile = x_pool.tile([P, TILES, FEATURES], BF16, name="x_tile")
-            nc.sync.dma_start(
-                out=x_tile[:],
-                in_=x_rows[g * GROUP : (g + 1) * GROUP, :].rearrange("(p j) k -> p j k", j=TILES),
-            )
+            if g == 2:
+                nc.sync.dma_start(out=w_rows[:], in_=w_o.rearrange("(c p) k -> p c k", p=P))
+            x_tile = x_pool.tile([P, tiles_of[g], FEATURES], BF16, name="x_tile_%d" % g)
+            nc.sync.dma_start(out=x_tile[:], in_=rows_of_group(x_rows, g))
             x_tiles.append(x_tile)
 
         ident = const.tile([P, P], F32)
         make_identity(nc, ident[:])
         half = const.tile([P, TILES], F32)
         nc.vector.memset(half[:], 0.5)
+        warm = const.tile([P, 1], F32)
+        nc.scalar.activation(out=warm[:], in_=half[:, 0:1], func=ACT.Silu)
 
         gate = const.tile([P, PACK], F32)
         size = const.tile([P, PACK], F32)
@@ -86,27 +98,29 @@ def tile_normlocalattention_pb_t_kernel(tc, attn_out, norm_scale, norm_gate, w_o
         nc.vector.reciprocal(out=gain[:], in_=gate[:])
         nc.vector.tensor_mul(out=gain[:], in0=gain[:], in1=scale_bf[:])
 
-        w_grouped = const.tile([P, OUT_FEATURES, 2], F32, align_bytes=64)
-        for h in range(2):
-            w_words = psum_words.tile([P, 2, 2 * P], F32, tag="words")
-            for u in range(2):
-                for c in range(2):
-                    nc.tensor.transpose(
-                        w_words[:, u, c * P : (c + 1) * P],
-                        w_rows[:, 2 * h + c, :].bitcast(F32)[:, u * P : (u + 1) * P],
-                        ident[:],
-                    )
-            nc.vector.tensor_copy(
-                out=w_grouped[:, h * 2 * P : (h + 1) * 2 * P, :],
-                in_=w_words[:].rearrange("p u o -> p o u"),
-            )
         w_codes = const.tile([P, OUT_FEATURES], U32, align_bytes=64)
         w_scales = const.tile([P, OUT_FEATURES], U8, align_bytes=64)
-        nc.vector.quantize_mx(
-            out=w_codes[:].bitcast(FP8X4),
-            scales=w_scales[:],
-            in_=w_grouped[:].rearrange("p o u -> p (o u)").bitcast(BF16),
-        )
+
+        def prepare_weights():
+            w_grouped = const.tile([P, OUT_FEATURES, 2], F32, align_bytes=64)
+            for h in range(2):
+                w_words = psum_acc.tile([P, 2, 2 * P], F32, name="w_words", tag="acc")
+                for u in range(2):
+                    for c in range(2):
+                        nc.tensor.transpose(
+                            w_words[:, u, c * P : (c + 1) * P],
+                            w_rows[:, 2 * h + c, :].bitcast(F32)[:, u * P : (u + 1) * P],
+                            ident[:],
+                        )
+                nc.vector.tensor_copy(
+                    out=w_grouped[:, h * 2 * P : (h + 1) * 2 * P, :],
+                    in_=w_words[:].rearrange("p u o -> p o u"),
+                )
+            nc.vector.quantize_mx(
+                out=w_codes[:].bitcast(FP8X4),
+                scales=w_scales[:],
+                in_=w_grouped[:].rearrange("p o u -> p (o u)").bitcast(BF16),
+            )
 
         rms_of = {}
         inv_all_of = {}
@@ -119,9 +133,10 @@ def tile_normlocalattention_pb_t_kernel(tc, attn_out, norm_scale, norm_gate, w_o
         acc_of = {}
 
         def root_mean_squares(g):
+            n = tiles_of[g]
             squares = work.tile([P, TILES, FEATURES], BF16, name="squares")
             mean_sq = stats.tile([P, TILES], F32, name="mean_sq")
-            for j in range(TILES):
+            for j in range(n):
                 nc.scalar.activation(
                     out=squares[:, j, :],
                     in_=x_tiles[g][:, j, :],
@@ -130,15 +145,18 @@ def tile_normlocalattention_pb_t_kernel(tc, attn_out, norm_scale, norm_gate, w_o
                     accum_out=mean_sq[:, j : j + 1],
                 )
             rms = stats.tile([P, TILES], F32, name="rms")
-            nc.gpsimd.tensor_tensor(out=rms[:], in0=mean_sq[:], in1=half[:], op=ALU.pow)
-            nc.gpsimd.tensor_scalar(out=rms[:], in0=rms[:], scalar1=EPS, scalar2=1.0, op0=ALU.add, op1=ALU.mult)
+            nc.gpsimd.tensor_tensor(out=rms[:, :n], in0=mean_sq[:, :n], in1=half[:, :n], op=ALU.pow)
+            nc.gpsimd.tensor_scalar(
+                out=rms[:, :n], in0=rms[:, :n], scalar1=EPS, scalar2=1.0, op0=ALU.add, op1=ALU.mult
+            )
             rms_of[g] = rms
 
         def spread_inverse_rms(g):
+            n = tiles_of[g]
             inv = stats.tile([P, TILES], F32, name="inv")
-            nc.vector.reciprocal(out=inv[:], in_=rms_of[g][:])
+            nc.vector.reciprocal(out=inv[:, :n], in_=rms_of[g][:, :n])
             inv_all = psum_inv.tile([P, GROUP], F32, name="inv_all")
-            for j in range(TILES):
+            for j in range(n):
                 nc.tensor.transpose(
                     inv_all[:, j * P : (j + 1) * P], inv[:, j : j + 1].to_broadcast([P, P]), ident[:]
                 )
@@ -146,8 +164,8 @@ def tile_normlocalattention_pb_t_kernel(tc, attn_out, norm_scale, norm_gate, w_o
 
         def transpose_x(g):
             for u in range(2):
-                x_words = psum_words.tile([P, GROUP], F32, name="x_words", tag="words")
-                for j in range(TILES):
+                x_words = psum_words.tile([P, GROUP], F32, name="x_words")
+                for j in range(tiles_of[g]):
                     nc.tensor.transpose(
                         x_words[:, j * P : (j + 1) * P],
                         x_tiles[g][:, j, :].bitcast(F32)[:, u * P : (u + 1) * P],
@@ -156,34 +174,37 @@ def tile_normlocalattention_pb_t_kernel(tc, attn_out, norm_scale, norm_gate, w_o
                 x_words_of[(g, u)] = x_words
 
         def gated(g):
+            width = tiles_of[g] * P
             silu = work.tile([P, PACK, GROUP], F32, name="silu")
             for u in range(2):
-                pairs = x_words_of[(g, u)][:].bitcast(BF16).rearrange("p (n e) -> p n e", e=2)
+                pairs = x_words_of[(g, u)][:, :width].bitcast(BF16).rearrange("p (m e) -> p m e", e=2)
                 for e in range(2):
                     t = 2 * u + e
                     nc.scalar.activation(
-                        out=silu[:, t, :], in_=pairs[:, :, e], func=ACT.Silu, scale=gate[:, t : t + 1]
+                        out=silu[:, t, :width], in_=pairs[:, :, e], func=ACT.Silu, scale=gate[:, t : t + 1]
                     )
             silu_of[g] = silu
 
         def normed(g):
+            width = tiles_of[g] * P
             y_planes = work.tile([P, PACK, GROUP], BF16, name="y_planes")
             for t in range(PACK):
                 nc.vector.scalar_tensor_tensor(
-                    out=y_planes[:, t, :],
-                    in0=silu_of[g][:, t, :],
+                    out=y_planes[:, t, :width],
+                    in0=silu_of[g][:, t, :width],
                     scalar=gain[:, t : t + 1],
-                    in1=inv_all_of[g][:],
+                    in1=inv_all_of[g][:, :width],
                     op0=ALU.mult,
                     op1=ALU.mult,
                 )
             y_planes_of[g] = y_planes
 
         def regroup(g):
+            width = tiles_of[g] * P
             y_grouped = single.tile([P, GROUP, PACK], BF16, name="y_grouped", align_bytes=64)
             nc.gpsimd.tensor_scalar(
-                out=y_grouped[:],
-                in0=y_planes_of[g][:].rearrange("p t n -> p n t"),
+                out=y_grouped[:, :width, :],
+                in0=y_planes_of[g][:, :, :width].rearrange("p t m -> p m t"),
                 scalar1=1.0,
                 scalar2=0.0,
                 op0=ALU.mult,
@@ -192,18 +213,19 @@ def tile_normlocalattention_pb_t_kernel(tc, attn_out, norm_scale, norm_gate, w_o
             y_grouped_of[g] = y_grouped
 
         def quantise(g):
+            width = tiles_of[g] * P
             y_codes = work.tile([P, GROUP], U32, name="y_codes", align_bytes=64)
             y_scales = work.tile([P, GROUP], U8, name="y_scales", align_bytes=64)
             nc.vector.quantize_mx(
-                out=y_codes[:].bitcast(FP8X4),
-                scales=y_scales[:],
-                in_=y_grouped_of[g][:].rearrange("p n t -> p (n t)"),
+                out=y_codes[:, :width].bitcast(FP8X4),
+                scales=y_scales[:, :width],
+                in_=y_grouped_of[g][:, :width, :].rearrange("p m t -> p (m t)"),
             )
             y_codes_of[g] = y_codes
             y_scales_of[g] = y_scales
 
         def multiply(g):
-            for j in range(TILES):
+            for j in range(tiles_of[g]):
                 acc = psum_acc.tile([P, OUT_FEATURES], F32, name="acc")
                 nc.tensor.matmul_mx(
                     out=acc[:],
@@ -217,13 +239,10 @@ def tile_normlocalattention_pb_t_kernel(tc, attn_out, norm_scale, norm_gate, w_o
                 acc_of[(g, j)] = acc
 
         def add_bias_and_store(g):
-            result = results.tile([P, TILES, OUT_FEATURES], F32, name="result")
-            for j in range(TILES):
-                nc.vector.tensor_tensor(out=result[:, j, :], in0=acc_of[(g, j)][:], in1=bias[:], op=ALU.add)
-            nc.sync.dma_start(
-                out=out_rows[g * GROUP : (g + 1) * GROUP, :].rearrange("(p j) o -> p j o", j=TILES),
-                in_=result[:],
-            )
+            for j in range(tiles_of[g]):
+                result = results.tile([P, OUT_FEATURES], F32, name="result")
+                nc.vector.tensor_tensor(out=result[:], in0=acc_of[(g, j)][:], in1=bias[:], op=ALU.add)
+                nc.sync.dma_start(out=rows_of_group(out_rows, g)[:, j, :], in_=result[:])
 
         def run(stage, g):
             if 0 <= g < groups:
@@ -235,6 +254,8 @@ def tile_normlocalattention_pb_t_kernel(tc, attn_out, norm_scale, norm_gate, w_o
             run(root_mean_squares, step + 2)
             run(normed, step)
             run(spread_inverse_rms, step + 1)
+            if step == 0:
+                prepare_weights()
             run(add_bias_and_store, step - 2)
             run(quantise, step - 1)
             run(multiply, step - 1)

@@ -20,28 +20,19 @@ FEATURES = P * PACK
 OUT_FEATURES = 512
 TILES = 4
 GROUP = TILES * P
-RAMP = (1, 1, 2)
+VECTOR_SUMS = 2
 EPS = 1e-8
 GATE_FLOOR = 2.0**-64
-
-
-def group_sizes(token_tiles):
-    full_groups = (token_tiles - 2 * sum(RAMP)) // TILES
-    sizes = list(RAMP) + [TILES] * full_groups + list(reversed(RAMP))
-    assert sum(sizes) == token_tiles
-    return sizes
 
 
 def tile_normlocalattention_pb_t_kernel(tc, attn_out, norm_scale, norm_gate, w_o, b_o, out):
     nc = tc.nc
     x_rows = attn_out.flatten_outer_dims()
     out_rows = out.flatten_outer_dims()
-    tiles_of = group_sizes(x_rows.shape[0] // P)
-    groups = len(tiles_of)
+    groups = x_rows.shape[0] // GROUP
 
     def rows_of_group(rows, g):
-        start = P * sum(tiles_of[:g])
-        return rows[start : start + P * tiles_of[g], :].rearrange("(p j) k -> p j k", j=tiles_of[g])
+        return rows[g * GROUP : (g + 1) * GROUP, :].rearrange("(p j) k -> p j k", j=TILES)
 
     with ExitStack() as stack:
         stack.enter_context(tc.manual_schedule())
@@ -50,7 +41,7 @@ def tile_normlocalattention_pb_t_kernel(tc, attn_out, norm_scale, norm_gate, w_o
         stats = stack.enter_context(tc.tile_pool(name="stats", bufs=4))
         work = stack.enter_context(tc.tile_pool(name="work", bufs=3))
         single = stack.enter_context(tc.tile_pool(name="single", bufs=1))
-        results = stack.enter_context(tc.tile_pool(name="results", bufs=2 * TILES))
+        results = stack.enter_context(tc.tile_pool(name="results", bufs=3))
         psum_words = stack.enter_context(tc.psum_pool(name="psum_words", bufs=3))
         psum_inv = stack.enter_context(tc.psum_pool(name="psum_inv", bufs=1))
         psum_acc = stack.enter_context(tc.psum_pool(name="psum_acc", bufs=TILES))
@@ -65,17 +56,17 @@ def tile_normlocalattention_pb_t_kernel(tc, attn_out, norm_scale, norm_gate, w_o
             out=scale_bf[:].rearrange("p (u e) -> p u e", e=2),
             in_=norm_scale.rearrange("(u p e) -> p u e", u=2, e=2),
         )
-        bias = const.tile([P, OUT_FEATURES], BF16)
-        nc.scalar.dma_start(out=bias[:], in_=b_o.partition_broadcast(P))
-
-        x_tiles = []
+        x_tiles = [x_pool.tile([P, TILES, FEATURES], BF16, name="x_tile_%d" % g) for g in range(groups)]
         w_rows = const.tile([P, OUT_FEATURES // P, FEATURES], BF16)
-        for g in range(groups):
-            if g == 2:
-                nc.sync.dma_start(out=w_rows[:], in_=w_o.rearrange("(c p) k -> p c k", p=P))
-            x_tile = x_pool.tile([P, tiles_of[g], FEATURES], BF16, name="x_tile_%d" % g)
-            nc.sync.dma_start(out=x_tile[:], in_=rows_of_group(x_rows, g))
-            x_tiles.append(x_tile)
+        bias = const.tile([P, OUT_FEATURES], BF16)
+        for j in range(TILES):
+            nc.sync.dma_start(out=x_tiles[0][:, j, :], in_=rows_of_group(x_rows, 0)[:, j, :])
+        nc.sync.dma_start(out=x_tiles[1][:], in_=rows_of_group(x_rows, 1))
+        nc.sync.dma_start(out=w_rows[:], in_=w_o.rearrange("(c p) k -> p c k", p=P))
+        nc.sync.dma_start(out=x_tiles[2][:], in_=rows_of_group(x_rows, 2))
+        nc.sync.dma_start(out=bias[:], in_=b_o.partition_broadcast(P))
+        for g in range(3, groups):
+            nc.sync.dma_start(out=x_tiles[g][:], in_=rows_of_group(x_rows, g))
 
         ident = const.tile([P, P], F32)
         make_identity(nc, ident[:])
@@ -133,30 +124,37 @@ def tile_normlocalattention_pb_t_kernel(tc, attn_out, norm_scale, norm_gate, w_o
         acc_of = {}
 
         def root_mean_squares(g):
-            n = tiles_of[g]
             squares = work.tile([P, TILES, FEATURES], BF16, name="squares")
             mean_sq = stats.tile([P, TILES], F32, name="mean_sq")
-            for j in range(n):
-                nc.scalar.activation(
-                    out=squares[:, j, :],
-                    in_=x_tiles[g][:, j, :],
-                    func=ACT.Square,
-                    scale=1.0 / math.sqrt(FEATURES),
-                    accum_out=mean_sq[:, j : j + 1],
-                )
+            for j in range(TILES):
+                if g < VECTOR_SUMS:
+                    nc.vector.scalar_tensor_tensor(
+                        out=squares[:, j, :],
+                        in0=x_tiles[g][:, j, :],
+                        scalar=1.0 / FEATURES,
+                        in1=x_tiles[g][:, j, :],
+                        op0=ALU.mult,
+                        op1=ALU.mult,
+                        accum_out=mean_sq[:, j : j + 1],
+                    )
+                else:
+                    nc.scalar.activation(
+                        out=squares[:, j, :],
+                        in_=x_tiles[g][:, j, :],
+                        func=ACT.Square,
+                        scale=1.0 / math.sqrt(FEATURES),
+                        accum_out=mean_sq[:, j : j + 1],
+                    )
             rms = stats.tile([P, TILES], F32, name="rms")
-            nc.gpsimd.tensor_tensor(out=rms[:, :n], in0=mean_sq[:, :n], in1=half[:, :n], op=ALU.pow)
-            nc.gpsimd.tensor_scalar(
-                out=rms[:, :n], in0=rms[:, :n], scalar1=EPS, scalar2=1.0, op0=ALU.add, op1=ALU.mult
-            )
+            nc.gpsimd.tensor_tensor(out=rms[:], in0=mean_sq[:], in1=half[:], op=ALU.pow)
+            nc.gpsimd.tensor_scalar(out=rms[:], in0=rms[:], scalar1=EPS, scalar2=1.0, op0=ALU.add, op1=ALU.mult)
             rms_of[g] = rms
 
         def spread_inverse_rms(g):
-            n = tiles_of[g]
             inv = stats.tile([P, TILES], F32, name="inv")
-            nc.vector.reciprocal(out=inv[:, :n], in_=rms_of[g][:, :n])
+            nc.vector.reciprocal(out=inv[:], in_=rms_of[g][:])
             inv_all = psum_inv.tile([P, GROUP], F32, name="inv_all")
-            for j in range(n):
+            for j in range(TILES):
                 nc.tensor.transpose(
                     inv_all[:, j * P : (j + 1) * P], inv[:, j : j + 1].to_broadcast([P, P]), ident[:]
                 )
@@ -165,7 +163,7 @@ def tile_normlocalattention_pb_t_kernel(tc, attn_out, norm_scale, norm_gate, w_o
         def transpose_x(g):
             for u in range(2):
                 x_words = psum_words.tile([P, GROUP], F32, name="x_words")
-                for j in range(tiles_of[g]):
+                for j in range(TILES):
                     nc.tensor.transpose(
                         x_words[:, j * P : (j + 1) * P],
                         x_tiles[g][:, j, :].bitcast(F32)[:, u * P : (u + 1) * P],
@@ -174,37 +172,34 @@ def tile_normlocalattention_pb_t_kernel(tc, attn_out, norm_scale, norm_gate, w_o
                 x_words_of[(g, u)] = x_words
 
         def gated(g):
-            width = tiles_of[g] * P
             silu = work.tile([P, PACK, GROUP], F32, name="silu")
             for u in range(2):
-                pairs = x_words_of[(g, u)][:, :width].bitcast(BF16).rearrange("p (m e) -> p m e", e=2)
+                pairs = x_words_of[(g, u)][:].bitcast(BF16).rearrange("p (m e) -> p m e", e=2)
                 for e in range(2):
                     t = 2 * u + e
                     nc.scalar.activation(
-                        out=silu[:, t, :width], in_=pairs[:, :, e], func=ACT.Silu, scale=gate[:, t : t + 1]
+                        out=silu[:, t, :], in_=pairs[:, :, e], func=ACT.Silu, scale=gate[:, t : t + 1]
                     )
             silu_of[g] = silu
 
         def normed(g):
-            width = tiles_of[g] * P
             y_planes = work.tile([P, PACK, GROUP], BF16, name="y_planes")
             for t in range(PACK):
                 nc.vector.scalar_tensor_tensor(
-                    out=y_planes[:, t, :width],
-                    in0=silu_of[g][:, t, :width],
+                    out=y_planes[:, t, :],
+                    in0=silu_of[g][:, t, :],
                     scalar=gain[:, t : t + 1],
-                    in1=inv_all_of[g][:, :width],
+                    in1=inv_all_of[g][:],
                     op0=ALU.mult,
                     op1=ALU.mult,
                 )
             y_planes_of[g] = y_planes
 
         def regroup(g):
-            width = tiles_of[g] * P
             y_grouped = single.tile([P, GROUP, PACK], BF16, name="y_grouped", align_bytes=64)
             nc.gpsimd.tensor_scalar(
-                out=y_grouped[:, :width, :],
-                in0=y_planes_of[g][:, :, :width].rearrange("p t m -> p m t"),
+                out=y_grouped[:],
+                in0=y_planes_of[g][:].rearrange("p t m -> p m t"),
                 scalar1=1.0,
                 scalar2=0.0,
                 op0=ALU.mult,
@@ -213,19 +208,18 @@ def tile_normlocalattention_pb_t_kernel(tc, attn_out, norm_scale, norm_gate, w_o
             y_grouped_of[g] = y_grouped
 
         def quantise(g):
-            width = tiles_of[g] * P
             y_codes = work.tile([P, GROUP], U32, name="y_codes", align_bytes=64)
             y_scales = work.tile([P, GROUP], U8, name="y_scales", align_bytes=64)
             nc.vector.quantize_mx(
-                out=y_codes[:, :width].bitcast(FP8X4),
-                scales=y_scales[:, :width],
-                in_=y_grouped_of[g][:, :width, :].rearrange("p m t -> p (m t)"),
+                out=y_codes[:].bitcast(FP8X4),
+                scales=y_scales[:],
+                in_=y_grouped_of[g][:].rearrange("p m t -> p (m t)"),
             )
             y_codes_of[g] = y_codes
             y_scales_of[g] = y_scales
 
         def multiply(g):
-            for j in range(tiles_of[g]):
+            for j in range(TILES):
                 acc = psum_acc.tile([P, OUT_FEATURES], F32, name="acc")
                 nc.tensor.matmul_mx(
                     out=acc[:],
@@ -239,10 +233,10 @@ def tile_normlocalattention_pb_t_kernel(tc, attn_out, norm_scale, norm_gate, w_o
                 acc_of[(g, j)] = acc
 
         def add_bias_and_store(g):
-            for j in range(tiles_of[g]):
-                result = results.tile([P, OUT_FEATURES], F32, name="result")
-                nc.vector.tensor_tensor(out=result[:], in0=acc_of[(g, j)][:], in1=bias[:], op=ALU.add)
-                nc.sync.dma_start(out=rows_of_group(out_rows, g)[:, j, :], in_=result[:])
+            result = results.tile([P, TILES, OUT_FEATURES], F32, name="result")
+            for j in range(TILES):
+                nc.vector.tensor_tensor(out=result[:, j, :], in0=acc_of[(g, j)][:], in1=bias[:], op=ALU.add)
+                nc.sync.dma_start(out=rows_of_group(out_rows, g)[:, j, :], in_=result[:, j, :])
 
         def run(stage, g):
             if 0 <= g < groups:
@@ -256,7 +250,7 @@ def tile_normlocalattention_pb_t_kernel(tc, attn_out, norm_scale, norm_gate, w_o
             run(spread_inverse_rms, step + 1)
             if step == 0:
                 prepare_weights()
-            run(add_bias_and_store, step - 2)
             run(quantise, step - 1)
             run(multiply, step - 1)
+            run(add_bias_and_store, step - 2)
             run(regroup, step)

from contextlib import ExitStack
import math

import concourse.mybir as mybir
from concourse.masks import make_identity

FLOPS = 2 * 8192 * 512 * 512

BF16 = mybir.dt.bfloat16
F32 = mybir.dt.float32
U32 = mybir.dt.uint32
U8 = mybir.dt.uint8
FP8X4 = mybir.dt.float8_e4m3fn_x4
ACT = mybir.ActivationFunctionType
ALU = mybir.AluOpType

P = 128
PACK = 4
FEATURES = P * PACK
OUT_FEATURES = 512
TILES = 4
GROUP = TILES * P
VECTOR_SUMS = 2
EPS = 1e-8
GATE_FLOOR = 2.0**-64


def tile_normlocalattention_pb_t_kernel(tc, attn_out, norm_scale, norm_gate, w_o, b_o, out):
    nc = tc.nc
    x_rows = attn_out.flatten_outer_dims()
    out_rows = out.flatten_outer_dims()
    groups = x_rows.shape[0] // GROUP

    def rows_of_group(rows, g):
        return rows[g * GROUP : (g + 1) * GROUP, :].rearrange("(p j) k -> p j k", j=TILES)

    with ExitStack() as stack:
        stack.enter_context(tc.manual_schedule())
        const = stack.enter_context(tc.tile_pool(name="const", bufs=1))
        x_pool = stack.enter_context(tc.tile_pool(name="x", bufs=1))
        stats = stack.enter_context(tc.tile_pool(name="stats", bufs=4))
        work = stack.enter_context(tc.tile_pool(name="work", bufs=3))
        single = stack.enter_context(tc.tile_pool(name="single", bufs=1))
        results = stack.enter_context(tc.tile_pool(name="results", bufs=3))
        psum_words = stack.enter_context(tc.psum_pool(name="psum_words", bufs=3))
        psum_inv = stack.enter_context(tc.psum_pool(name="psum_inv", bufs=1))
        psum_acc = stack.enter_context(tc.psum_pool(name="psum_acc", bufs=TILES))

        gate_bf = const.tile([P, PACK], BF16)
        scale_bf = const.tile([P, PACK], BF16)
        nc.scalar.dma_start(
            out=gate_bf[:].rearrange("p (u e) -> p u e", e=2),
            in_=norm_gate.rearrange("(u p e) -> p u e", u=2, e=2),
        )
        nc.scalar.dma_start(
            out=scale_bf[:].rearrange("p (u e) -> p u e", e=2),
            in_=norm_scale.rearrange("(u p e) -> p u e", u=2, e=2),
        )
        x_tiles = [x_pool.tile([P, TILES, FEATURES], BF16, name="x_tile_%d" % g) for g in range(groups)]
        w_rows = const.tile([P, OUT_FEATURES // P, FEATURES], BF16)
        bias = const.tile([P, OUT_FEATURES], BF16)
        for j in range(TILES):
            nc.sync.dma_start(out=x_tiles[0][:, j, :], in_=rows_of_group(x_rows, 0)[:, j, :])
        nc.sync.dma_start(out=x_tiles[1][:], in_=rows_of_group(x_rows, 1))
        nc.sync.dma_start(out=w_rows[:], in_=w_o.rearrange("(c p) k -> p c k", p=P))
        nc.sync.dma_start(out=x_tiles[2][:], in_=rows_of_group(x_rows, 2))
        nc.sync.dma_start(out=bias[:], in_=b_o.partition_broadcast(P))
        for g in range(3, groups):
            nc.sync.dma_start(out=x_tiles[g][:], in_=rows_of_group(x_rows, g))

        ident = const.tile([P, P], F32)
        make_identity(nc, ident[:])
        half = const.tile([P, TILES], F32)
        nc.vector.memset(half[:], 0.5)
        warm = const.tile([P, 1], F32)
        nc.scalar.activation(out=warm[:], in_=half[:, 0:1], func=ACT.Silu)

        gate = const.tile([P, PACK], F32)
        size = const.tile([P, PACK], F32)
        lift = const.tile([P, PACK], F32)
        gain = const.tile([P, PACK], F32)
        nc.vector.tensor_copy(out=gate[:], in_=gate_bf[:])
        nc.vector.tensor_scalar_mul(out=size[:], in0=gate[:], scalar1=-1.0)
        nc.vector.tensor_max(out=size[:], in0=size[:], in1=gate[:])
        nc.vector.tensor_scalar(
            out=lift[:], in0=size[:], scalar1=GATE_FLOOR, scalar2=GATE_FLOOR, op0=ALU.is_lt, op1=ALU.mult
        )
        nc.vector.tensor_add(out=gate[:], in0=gate[:], in1=lift[:])
        nc.vector.reciprocal(out=gain[:], in_=gate[:])
        nc.vector.tensor_mul(out=gain[:], in0=gain[:], in1=scale_bf[:])

        w_codes = const.tile([P, OUT_FEATURES], U32, align_bytes=64)
        w_scales = const.tile([P, OUT_FEATURES], U8, align_bytes=64)

        def prepare_weights():
            w_grouped = const.tile([P, OUT_FEATURES, 2], F32, align_bytes=64)
            for h in range(2):
                w_words = psum_acc.tile([P, 2, 2 * P], F32, name="w_words", tag="acc")
                for u in range(2):
                    for c in range(2):
                        nc.tensor.transpose(
                            w_words[:, u, c * P : (c + 1) * P],
                            w_rows[:, 2 * h + c, :].bitcast(F32)[:, u * P : (u + 1) * P],
                            ident[:],
                        )
                nc.vector.tensor_copy(
                    out=w_grouped[:, h * 2 * P : (h + 1) * 2 * P, :],
                    in_=w_words[:].rearrange("p u o -> p o u"),
                )
            nc.vector.quantize_mx(
                out=w_codes[:].bitcast(FP8X4),
                scales=w_scales[:],
                in_=w_grouped[:].rearrange("p o u -> p (o u)").bitcast(BF16),
            )

        rms_of = {}
        inv_all_of = {}
        x_words_of = {}
        silu_of = {}
        y_planes_of = {}
        y_grouped_of = {}
        y_codes_of = {}
        y_scales_of = {}
        acc_of = {}

        def root_mean_squares(g):
            squares = work.tile([P, TILES, FEATURES], BF16, name="squares")
            mean_sq = stats.tile([P, TILES], F32, name="mean_sq")
            for j in range(TILES):
                if g < VECTOR_SUMS:
                    nc.vector.scalar_tensor_tensor(
                        out=squares[:, j, :],
                        in0=x_tiles[g][:, j, :],
                        scalar=1.0 / FEATURES,
                        in1=x_tiles[g][:, j, :],
                        op0=ALU.mult,
                        op1=ALU.mult,
                        accum_out=mean_sq[:, j : j + 1],
                    )
                else:
                    nc.scalar.activation(
                        out=squares[:, j, :],
                        in_=x_tiles[g][:, j, :],
                        func=ACT.Square,
                        scale=1.0 / math.sqrt(FEATURES),
                        accum_out=mean_sq[:, j : j + 1],
                    )
            rms = stats.tile([P, TILES], F32, name="rms")
            nc.gpsimd.tensor_tensor(out=rms[:], in0=mean_sq[:], in1=half[:], op=ALU.pow)
            nc.gpsimd.tensor_scalar(out=rms[:], in0=rms[:], scalar1=EPS, scalar2=1.0, op0=ALU.add, op1=ALU.mult)
            rms_of[g] = rms

        def spread_inverse_rms(g):
            inv = stats.tile([P, TILES], F32, name="inv")
            nc.vector.reciprocal(out=inv[:], in_=rms_of[g][:])
            inv_all = psum_inv.tile([P, GROUP], F32, name="inv_all")
            for j in range(TILES):
                nc.tensor.transpose(
                    inv_all[:, j * P : (j + 1) * P], inv[:, j : j + 1].to_broadcast([P, P]), ident[:]
                )
            inv_all_of[g] = inv_all

        def transpose_x(g):
            for u in range(2):
                x_words = psum_words.tile([P, GROUP], F32, name="x_words")
                for j in range(TILES):
                    nc.tensor.transpose(
                        x_words[:, j * P : (j + 1) * P],
                        x_tiles[g][:, j, :].bitcast(F32)[:, u * P : (u + 1) * P],
                        ident[:],
                    )
                x_words_of[(g, u)] = x_words

        def gated(g):
            silu = work.tile([P, PACK, GROUP], F32, name="silu")
            for u in range(2):
                pairs = x_words_of[(g, u)][:].bitcast(BF16).rearrange("p (m e) -> p m e", e=2)
                for e in range(2):
                    t = 2 * u + e
                    nc.scalar.activation(
                        out=silu[:, t, :], in_=pairs[:, :, e], func=ACT.Silu, scale=gate[:, t : t + 1]
                    )
            silu_of[g] = silu

        def normed(g):
            y_planes = work.tile([P, PACK, GROUP], BF16, name="y_planes")
            for t in range(PACK):
                nc.vector.scalar_tensor_tensor(
                    out=y_planes[:, t, :],
                    in0=silu_of[g][:, t, :],
                    scalar=gain[:, t : t + 1],
                    in1=inv_all_of[g][:],
                    op0=ALU.mult,
                    op1=ALU.mult,
                )
            y_planes_of[g] = y_planes

        def regroup(g):
            y_grouped = single.tile([P, GROUP, PACK], BF16, name="y_grouped", align_bytes=64)
            nc.gpsimd.tensor_scalar(
                out=y_grouped[:],
                in0=y_planes_of[g][:].rearrange("p t m -> p m t"),
                scalar1=1.0,
                scalar2=0.0,
                op0=ALU.mult,
                op1=ALU.add,
            )
            y_grouped_of[g] = y_grouped

        def quantise(g):
            y_codes = work.tile([P, GROUP], U32, name="y_codes", align_bytes=64)
            y_scales = work.tile([P, GROUP], U8, name="y_scales", align_bytes=64)
            nc.vector.quantize_mx(
                out=y_codes[:].bitcast(FP8X4),
                scales=y_scales[:],
                in_=y_grouped_of[g][:].rearrange("p m t -> p (m t)"),
            )
            y_codes_of[g] = y_codes
            y_scales_of[g] = y_scales

        def multiply(g):
            for j in range(TILES):
                acc = psum_acc.tile([P, OUT_FEATURES], F32, name="acc")
                nc.tensor.matmul_mx(
                    out=acc[:],
                    lhsT=y_codes_of[g][:, j * P : (j + 1) * P].bitcast(FP8X4),
                    lhsT_scale=y_scales_of[g][:, j * P : (j + 1) * P],
                    rhs=w_codes[:].bitcast(FP8X4),
                    rhs_scale=w_scales[:],
                    start=True,
                    stop=True,
                )
                acc_of[(g, j)] = acc

        def add_bias_and_store(g):
            result = results.tile([P, TILES, OUT_FEATURES], F32, name="result")
            for j in range(TILES):
                nc.vector.tensor_tensor(out=result[:, j, :], in0=acc_of[(g, j)][:], in1=bias[:], op=ALU.add)
                nc.sync.dma_start(out=rows_of_group(out_rows, g)[:, j, :], in_=result[:, j, :])

        def run(stage, g):
            if 0 <= g < groups:
                stage(g)

        for step in range(-2, groups + 2):
            run(gated, step + 1)
            run(transpose_x, step + 2)
            run(root_mean_squares, step + 2)
            run(normed, step)
            run(spread_inverse_rms, step + 1)
            if step == 0:
                prepare_weights()
            run(quantise, step - 1)
            run(multiply, step - 1)
            run(add_bias_and_store, step - 2)
            run(regroup, step)
